import numpy as np
import ml_dtypes


def mxq(x, axis, fmt="e4m3"):
    dtype, down = {"e4m3": (ml_dtypes.float8_e4m3fn, 7), "e5m2": (ml_dtypes.float8_e5m2, 14)}[fmt]
    v = np.moveaxis(np.asarray(x, np.float32).astype(ml_dtypes.bfloat16).astype(np.float64), axis, -1)
    blocks = v.reshape(v.shape[:-1] + (-1, 32))
    amax = np.abs(blocks).max(-1, keepdims=True)
    byte = np.maximum(np.where(amax > 0, np.frexp(amax)[1] - 1 + 127, 0) - down, 1)
    scale = np.exp2(byte - 127.0)
    codes = (blocks / scale).astype(np.float32).astype(dtype).astype(np.float64)
    return np.moveaxis((codes * scale).reshape(v.shape), -1, axis)


WIDE = False


def mx_kscale(k):
    if not WIDE:
        return np.ones(k)
    levels = np.array([10, -10, 5, -5, 0])
    a = np.random.permutation(np.resize(levels, k // 512 * 4)).reshape(k // 512, 4)
    idx = np.arange(k)
    return np.exp2(a[idx // 512, idx % 128 // 32])


BF16 = ml_dtypes.bfloat16


def bf(x):
    return np.asarray(x, np.float32).astype(BF16)


def f64(x):
    return np.asarray(x).astype(np.float64)


E2M1 = np.array([0.0, 0.5, 1.0, 1.5, 2.0, 3.0, 4.0, 6.0, -0.0, -0.5, -1.0, -1.5, -2.0, -3.0, -4.0, -6.0])


def pack_weight(w, fmt):
    k, n = w.shape
    w = f64(bf(w)).reshape(k // 32, 32, n)
    amax = np.abs(w).max(1)
    if fmt == "e4m3":
        byte = np.frexp(amax)[1] - 1 + 127 - 7
    else:
        mant, ex = np.frexp(amax / 6.0)
        byte = np.where(mant > 0.5, ex, ex - 1) + 127
    byte = np.clip(np.where(amax > 0, byte, 1), 1, 254)
    scaled = (w * np.exp2(127.0 - byte)[:, None, :]).reshape(k, n).astype(np.float32)
    by_word = np.ascontiguousarray(scaled.reshape(k // 512, 128, 4, n).transpose(0, 1, 3, 2))
    if fmt == "e4m3":
        words = by_word.astype(ml_dtypes.float8_e4m3fn).view(np.uint8)
    else:
        c = by_word.astype(ml_dtypes.float4_e2m1fn).view(np.uint8) & 0xF
        words = c[..., 0::2] | (c[..., 1::2] << 4)
    return np.ascontiguousarray(words), np.ascontiguousarray(byte.astype(np.uint8).reshape(k // 512, 16, n))


def unpack_weight(words, scales, fmt):
    g, p, n, _ = words.shape
    if fmt == "e4m3":
        vals = np.ascontiguousarray(words).view(ml_dtypes.float8_e4m3fn).astype(np.float64)
    else:
        nib = np.empty((g, p, n, 4), np.uint8)
        nib[..., 0::2] = words & 0xF
        nib[..., 1::2] = words >> 4
        vals = E2M1[nib]
    vals = vals * np.repeat(np.exp2(scales.astype(np.float64) - 127.0), 8, axis=1)[..., None]
    return vals.transpose(0, 1, 3, 2).reshape(g * 512, n)


B, S, D_IN, D_OUT = 2, 64, 4096, 2048


def quant8(w):
    mv = np.max(np.abs(w))
    q = np.ceil(np.log2(mv)) - 6.0
    scale = np.exp2(q)
    return np.round(w / scale) * scale


def setup_inputs():
    s = mx_kscale(D_IN)
    x = np.random.standard_normal((B, S, D_IN))
    weight = np.random.standard_normal((D_OUT, D_IN)) * 3.0 / np.sqrt(D_IN)
    w_upper = quant8(weight)
    w_lower = weight - w_upper
    upper_words, upper_scales = pack_weight((w_upper / s[None, :]).T, "e4m3")
    lower_words, lower_scales = pack_weight((w_lower / s[None, :]).T, "e4m3")
    return {"x": bf(x * s), "weight_upper_words": upper_words, "weight_upper_scales": upper_scales, "weight_lower_words": lower_words, "weight_lower_scales": lower_scales}


def reference(x, weight_upper_words, weight_upper_scales, weight_lower_words, weight_lower_scales):
    xq = mxq(f64(x), 2, "e4m3")
    y_upper = xq @ unpack_weight(weight_upper_words, weight_upper_scales, "e4m3")
    y_lower = xq @ unpack_weight(weight_lower_words, weight_lower_scales, "e4m3")
    return y_upper + y_lower

@@ -1,0 +1,123 @@
+from contextlib import ExitStack
+
+import concourse.mybir as mybir
+from concourse.masks import make_identity
+
+F32 = mybir.dt.float32
+BF16 = mybir.dt.bfloat16
+I32 = mybir.dt.int32
+U32 = mybir.dt.uint32
+U8 = mybir.dt.uint8
+FP8X4 = mybir.dt.float8_e4m3fn_x4
+
+P = 128
+K = 4096
+N = 2048
+GROUPS = K // 512
+NT = 512
+COLS = N // NT
+FLOPS = 2 * 2 * P * K * N
+
+SCALE_QUEUE = "sync"
+SPLIT_LAST = True
+
+
+def tile_virtual16bmatmul_w_kernel(
+    tc, x, weight_upper_words, weight_upper_scales, weight_lower_words, weight_lower_scales, out
+):
+    nc = tc.nc
+    x_rows = x.flatten_outer_dims()
+    out_rows = out.flatten_outer_dims()
+    words = [weight_upper_words, weight_lower_words]
+    scales = [weight_upper_scales, weight_lower_scales]
+    chunks = [(w, 4 * h + j) for h in range(2) for w in range(2) for j in range(4)]
+
+    with ExitStack() as ctx:
+        keep = ctx.enter_context(tc.tile_pool(name="keep", bufs=1))
+        psum = ctx.enter_context(tc.psum_pool(name="psum", bufs=1))
+        ctx.enter_context(tc.manual_schedule())
+
+        planes = keep.tile([P, 4 * N], U8, name="planes", align_bytes=64)
+        nc.vector.memset(planes[:].bitcast(I32), 0)
+        ident = keep.tile([P, P], F32, name="ident")
+        make_identity(nc, ident[:])
+
+        x_sb = keep.tile([P, K], BF16, name="x_sb", align_bytes=64)
+        nc.sync.dma_start(out=x_sb[:], in_=x_rows)
+
+        for h in range(2):
+            for w in range(2):
+                i = 2 * h + w
+                for q in range(4):
+                    dst = planes[32 * q : 32 * q + 16, N * i : N * (i + 1)]
+                    src = scales[w][4 * h : 4 * h + 4, 4 * q : 4 * q + 4, :]
+                    if SCALE_QUEUE == "sync":
+                        nc.sync.dma_start(out=dst.bitcast(I32), in_=src.bitcast(I32))
+                    else:
+                        nc.gpsimd.dma_start(out=dst.bitcast(F32), in_=src.bitcast(F32))
+
+        w_tiles = {}
+        for n_chunk, (w, g) in enumerate(chunks):
+            src = words[w][g].rearrange("p n t -> p (n t)")
+            if SPLIT_LAST and n_chunk == len(chunks) - 1:
+                for c in range(COLS):
+                    piece = keep.tile([P, 4 * NT], U8, name="wq%d" % c, align_bytes=64)
+                    nc.sync.dma_start(
+                        out=piece[:].bitcast(I32), in_=src[:, 4 * NT * c : 4 * NT * (c + 1)].bitcast(I32)
+                    )
+                    w_tiles[(w, g, c)] = piece[:]
+            else:
+                whole = keep.tile([P, 4 * N], U8, name="w%d_%d" % (w, g), align_bytes=64)
+                nc.sync.dma_start(out=whole[:].bitcast(I32), in_=src.bitcast(I32))
+                for c in range(COLS):
+                    w_tiles[(w, g, c)] = whole[:, 4 * NT * c : 4 * NT * (c + 1)]
+
+        x_words = x_sb[:].bitcast(F32)
+        grouped = keep.tile([P, K], BF16, name="grouped", align_bytes=64)
+        grouped_words = grouped[:].bitcast(F32).rearrange("p (g m u) -> p g m u", g=GROUPS, m=P, u=2)
+        x_codes = keep.tile([P, GROUPS * P], U32, name="x_codes", align_bytes=64)
+        x_scales = keep.tile([P, GROUPS * P], U8, name="x_scales", align_bytes=64)
+        banks = []
+        for b in range(4):
+            xt = psum.tile([P, 2, 2, P], F32, name="xt%d" % b)
+            banks.append(xt)
+            for gg in range(2):
+                g = 2 * b + gg
+                for u in range(2):
+                    nc.tensor.transpose(xt[:, gg, u, :], x_words[:, 256 * g + u : 256 * (g + 1) : 2], ident[:])
+        for b in (0, 2):
+            nc.vector.tensor_copy(
+                out=grouped_words[:, 2 * b : 2 * b + 2, :, :], in_=banks[b][:].rearrange("p g u m -> p g m u")
+            )
+        for b in (1, 3):
+            nc.scalar.copy(
+                out=grouped_words[:, 2 * b : 2 * b + 2, :, :], in_=banks[b][:].rearrange("p g u m -> p g m u")
+            )
+        for b in range(4):
+            nc.vector.quantize_mx(
+                out=x_codes[:, 256 * b : 256 * (b + 1)].bitcast(FP8X4),
+                scales=x_scales[:, 256 * b : 256 * (b + 1)],
+                in_=grouped[:, 1024 * b : 1024 * (b + 1)],
+            )
+
+        acc = [psum.tile([P, NT], F32, name="acc%d" % c) for c in range(COLS)]
+        for n_chunk, (w, g) in enumerate(chunks):
+            i = 2 * (g // 4) + w
+            k_off = 4 * (g % 4)
+            for c in range(COLS):
+                nc.tensor.matmul_mx(
+                    out=acc[c][:],
+                    lhsT=x_codes[:, P * g : P * (g + 1)].bitcast(FP8X4),
+                    lhsT_scale=x_scales[:, P * g : P * (g + 1)],
+                    rhs=w_tiles[(w, g, c)].bitcast(FP8X4),
+                    rhs_scale=planes[k_off:P, N * i + NT * c : N * i + NT * (c + 1)],
+                    start=(n_chunk == 0),
+                    stop=(n_chunk == len(chunks) - 1),
+                )
+        for c in range(COLS):
+            res = keep.tile([P, NT], F32, name="res%d" % c)
+            if c % 2 == 0:
+                nc.vector.tensor_copy(out=res[:], in_=acc[c][:])
+            else:
+                nc.scalar.copy(out=res[:], in_=acc[c][:])
+            nc.sync.dma_start(out=out_rows[:, NT * c : NT * (c + 1)], in_=res[:])

@@ -18,7 +18,7 @@ NT = 512
 COLS = N // NT
 FLOPS = 2 * 2 * P * K * N
 
-SCALE_QUEUE = "sync"
+SCALE_QUEUE = "gpsimd"
 SPLIT_LAST = True
 
 

@@ -37,12 +37,12 @@ def tile_virtual16bmatmul_w_kernel(
         psum = ctx.enter_context(tc.psum_pool(name="psum", bufs=1))
         ctx.enter_context(tc.manual_schedule())
 
-        planes = keep.tile([P, 4 * N], U8, name="planes", align_bytes=64)
+        planes = keep.tile([P, 4 * N], U8, name="planes", align_bytes=256)
         nc.vector.memset(planes[:].bitcast(I32), 0)
-        ident = keep.tile([P, P], F32, name="ident")
+        ident = keep.tile([P, P], F32, name="ident", align_bytes=256)
         make_identity(nc, ident[:])
 
-        x_sb = keep.tile([P, K], BF16, name="x_sb", align_bytes=64)
+        x_sb = keep.tile([P, K], BF16, name="x_sb", align_bytes=256)
         nc.sync.dma_start(out=x_sb[:], in_=x_rows)
 
         for h in range(2):
@@ -61,22 +61,22 @@ def tile_virtual16bmatmul_w_kernel(
             src = words[w][g].rearrange("p n t -> p (n t)")
             if SPLIT_LAST and n_chunk == len(chunks) - 1:
                 for c in range(COLS):
-                    piece = keep.tile([P, 4 * NT], U8, name="wq%d" % c, align_bytes=64)
+                    piece = keep.tile([P, 4 * NT], U8, name="wq%d" % c, align_bytes=256)
                     nc.sync.dma_start(
                         out=piece[:].bitcast(I32), in_=src[:, 4 * NT * c : 4 * NT * (c + 1)].bitcast(I32)
                     )
                     w_tiles[(w, g, c)] = piece[:]
             else:
-                whole = keep.tile([P, 4 * N], U8, name="w%d_%d" % (w, g), align_bytes=64)
+                whole = keep.tile([P, 4 * N], U8, name="w%d_%d" % (w, g), align_bytes=256)
                 nc.sync.dma_start(out=whole[:].bitcast(I32), in_=src.bitcast(I32))
                 for c in range(COLS):
                     w_tiles[(w, g, c)] = whole[:, 4 * NT * c : 4 * NT * (c + 1)]
 
         x_words = x_sb[:].bitcast(F32)
-        grouped = keep.tile([P, K], BF16, name="grouped", align_bytes=64)
+        grouped = keep.tile([P, K], BF16, name="grouped", align_bytes=256)
         grouped_words = grouped[:].bitcast(F32).rearrange("p (g m u) -> p g m u", g=GROUPS, m=P, u=2)
-        x_codes = keep.tile([P, GROUPS * P], U32, name="x_codes", align_bytes=64)
-        x_scales = keep.tile([P, GROUPS * P], U8, name="x_scales", align_bytes=64)
+        x_codes = keep.tile([P, GROUPS * P], U32, name="x_codes", align_bytes=256)
+        x_scales = keep.tile([P, GROUPS * P], U8, name="x_scales", align_bytes=256)
         banks = []
         for b in range(4):
             xt = psum.tile([P, 2, 2, P], F32, name="xt%d" % b)
@@ -115,7 +115,7 @@ def tile_virtual16bmatmul_w_kernel(
                     stop=(n_chunk == len(chunks) - 1),
                 )
         for c in range(COLS):
-            res = keep.tile([P, NT], F32, name="res%d" % c)
+            res = keep.tile([P, NT], F32, name="res%d" % c, align_bytes=256)
             if c % 2 == 0:
                 nc.vector.tensor_copy(out=res[:], in_=acc[c][:])
             else:

@@ -18,7 +18,6 @@ NT = 512
 COLS = N // NT
 FLOPS = 2 * 2 * P * K * N
 
-SCALE_QUEUE = "gpsimd"
 SPLIT_LAST = True
 
 
@@ -45,19 +44,21 @@ def tile_virtual16bmatmul_w_kernel(
         x_sb = keep.tile([P, K], BF16, name="x_sb", align_bytes=256)
         nc.sync.dma_start(out=x_sb[:], in_=x_rows)
 
+        def load_scales(h, w, quadrants, queue, view):
+            i = 2 * h + w
+            for q in quadrants:
+                dst = planes[32 * q : 32 * q + 16, N * i : N * (i + 1)]
+                src = scales[w][4 * h : 4 * h + 4, 4 * q : 4 * q + 4, :]
+                queue.dma_start(out=dst.bitcast(view), in_=src.bitcast(view))
+
         for h in range(2):
             for w in range(2):
-                i = 2 * h + w
-                for q in range(4):
-                    dst = planes[32 * q : 32 * q + 16, N * i : N * (i + 1)]
-                    src = scales[w][4 * h : 4 * h + 4, 4 * q : 4 * q + 4, :]
-                    if SCALE_QUEUE == "sync":
-                        nc.sync.dma_start(out=dst.bitcast(I32), in_=src.bitcast(I32))
-                    else:
-                        nc.gpsimd.dma_start(out=dst.bitcast(F32), in_=src.bitcast(F32))
+                load_scales(h, w, (2, 3), nc.gpsimd, F32)
 
         w_tiles = {}
         for n_chunk, (w, g) in enumerate(chunks):
+            if n_chunk % 4 == 1:
+                load_scales(g // 4, w, (0, 1), nc.sync, I32)
             src = words[w][g].rearrange("p n t -> p (n t)")
             if SPLIT_LAST and n_chunk == len(chunks) - 1:
                 for c in range(COLS):

@@ -57,7 +57,7 @@ def tile_virtual16bmatmul_w_kernel(
 
         w_tiles = {}
         for n_chunk, (w, g) in enumerate(chunks):
-            if n_chunk % 4 == 1:
+            if n_chunk == 2 or (n_chunk > 2 and n_chunk % 4 == 0):
                 load_scales(g // 4, w, (0, 1), nc.sync, I32)
             src = words[w][g].rearrange("p n t -> p (n t)")
             if SPLIT_LAST and n_chunk == len(chunks) - 1:

@@ -18,7 +18,9 @@ NT = 512
 COLS = N // NT
 FLOPS = 2 * 2 * P * K * N
 
-SPLIT_LAST = True
+UNITS = [(0, 512), (512, 512), (1024, 512), (1536, 256), (1792, 256)]
+TAIL_CHUNKS = 2
+TAIL = [(14, 0, 2), (15, 0, 2), (14, 2, 1), (15, 2, 1), (14, 3, 2), (15, 3, 1), (15, 4, 1)]
 
 
 def tile_virtual16bmatmul_w_kernel(
@@ -59,19 +61,23 @@ def tile_virtual16bmatmul_w_kernel(
         for n_chunk, (w, g) in enumerate(chunks):
             if n_chunk == 2 or (n_chunk > 2 and n_chunk % 4 == 0):
                 load_scales(g // 4, w, (0, 1), nc.sync, I32)
+            if n_chunk >= len(chunks) - TAIL_CHUNKS:
+                continue
             src = words[w][g].rearrange("p n t -> p (n t)")
-            if SPLIT_LAST and n_chunk == len(chunks) - 1:
-                for c in range(COLS):
-                    piece = keep.tile([P, 4 * NT], U8, name="wq%d" % c, align_bytes=256)
-                    nc.sync.dma_start(
-                        out=piece[:].bitcast(I32), in_=src[:, 4 * NT * c : 4 * NT * (c + 1)].bitcast(I32)
-                    )
-                    w_tiles[(w, g, c)] = piece[:]
-            else:
-                whole = keep.tile([P, 4 * N], U8, name="w%d_%d" % (w, g), align_bytes=256)
-                nc.sync.dma_start(out=whole[:].bitcast(I32), in_=src.bitcast(I32))
-                for c in range(COLS):
-                    w_tiles[(w, g, c)] = whole[:, 4 * NT * c : 4 * NT * (c + 1)]
+            whole = keep.tile([P, 4 * N], U8, name="w%d_%d" % (w, g), align_bytes=256)
+            nc.sync.dma_start(out=whole[:].bitcast(I32), in_=src.bitcast(I32))
+            for u, (c0, width) in enumerate(UNITS):
+                w_tiles[(n_chunk, u)] = whole[:, 4 * c0 : 4 * (c0 + width)]
+        for n_chunk, u0, count in TAIL:
+            w, g = chunks[n_chunk]
+            src = words[w][g].rearrange("p n t -> p (n t)")
+            first = UNITS[u0][0]
+            cols = sum(UNITS[u][1] for u in range(u0, u0 + count))
+            piece = keep.tile([P, 4 * cols], U8, name="wp%d_%d" % (n_chunk, u0), align_bytes=256)
+            nc.sync.dma_start(out=piece[:].bitcast(I32), in_=src[:, 4 * first : 4 * (first + cols)].bitcast(I32))
+            for u in range(u0, u0 + count):
+                c0, width = UNITS[u]
+                w_tiles[(n_chunk, u)] = piece[:, 4 * (c0 - first) : 4 * (c0 - first + width)]
 
         x_words = x_sb[:].bitcast(F32)
         grouped = keep.tile([P, K], BF16, name="grouped", align_bytes=256)
@@ -101,24 +107,34 @@ def tile_virtual16bmatmul_w_kernel(
                 in_=grouped[:, 1024 * b : 1024 * (b + 1)],
             )
 
-        acc = [psum.tile([P, NT], F32, name="acc%d" % c) for c in range(COLS)]
-        for n_chunk, (w, g) in enumerate(chunks):
+        acc = [psum.tile([P, UNITS[u][1]], F32, name="acc%d" % u) for u in range(4)]
+        acc.append(psum.tile([P, UNITS[4][1]], F32, name="acc4", tag="xt0"))
+
+        def multiply(n_chunk, u):
+            w, g = chunks[n_chunk]
             i = 2 * (g // 4) + w
             k_off = 4 * (g % 4)
-            for c in range(COLS):
-                nc.tensor.matmul_mx(
-                    out=acc[c][:],
-                    lhsT=x_codes[:, P * g : P * (g + 1)].bitcast(FP8X4),
-                    lhsT_scale=x_scales[:, P * g : P * (g + 1)],
-                    rhs=w_tiles[(w, g, c)].bitcast(FP8X4),
-                    rhs_scale=planes[k_off:P, N * i + NT * c : N * i + NT * (c + 1)],
-                    start=(n_chunk == 0),
-                    stop=(n_chunk == len(chunks) - 1),
-                )
-        for c in range(COLS):
-            res = keep.tile([P, NT], F32, name="res%d" % c, align_bytes=256)
-            if c % 2 == 0:
-                nc.vector.tensor_copy(out=res[:], in_=acc[c][:])
+            c0, width = UNITS[u]
+            nc.tensor.matmul_mx(
+                out=acc[u][:],
+                lhsT=x_codes[:, P * g : P * (g + 1)].bitcast(FP8X4),
+                lhsT_scale=x_scales[:, P * g : P * (g + 1)],
+                rhs=w_tiles[(n_chunk, u)].bitcast(FP8X4),
+                rhs_scale=planes[k_off:P, N * i + c0 : N * i + c0 + width],
+                start=(n_chunk == 0),
+                stop=(n_chunk == len(chunks) - 1),
+            )
+
+        for n_chunk in range(len(chunks) - TAIL_CHUNKS):
+            for u in range(len(UNITS)):
+                multiply(n_chunk, u)
+        for n_chunk, u0, count in TAIL:
+            for u in range(u0, u0 + count):
+                multiply(n_chunk, u)
+        for u, (c0, width) in enumerate(UNITS):
+            res = keep.tile([P, width], F32, name="res%d" % u, align_bytes=256)
+            if u % 2 == 0:
+                nc.vector.tensor_copy(out=res[:], in_=acc[u][:])
             else:
-                nc.scalar.copy(out=res[:], in_=acc[c][:])
-            nc.sync.dma_start(out=out_rows[:, NT * c : NT * (c + 1)], in_=res[:])
+                nc.scalar.copy(out=res[:], in_=acc[u][:])
+            nc.sync.dma_start(out=out_rows[:, c0 : c0 + width], in_=res[:])

@@ -20,6 +20,7 @@ FLOPS = 2 * 2 * P * K * N
 
 UNITS = [(0, 512), (512, 512), (1024, 512), (1536, 256), (1792, 256)]
 TAIL_CHUNKS = 2
+PAIRED = 12
 TAIL = [(14, 0, 2), (15, 0, 2), (14, 2, 1), (15, 2, 1), (14, 3, 2), (15, 3, 1), (15, 4, 1)]
 
 
@@ -62,6 +63,18 @@ def tile_virtual16bmatmul_w_kernel(
             if n_chunk == 2 or (n_chunk > 2 and n_chunk % 4 == 0):
                 load_scales(g // 4, w, (0, 1), nc.sync, I32)
             if n_chunk >= len(chunks) - TAIL_CHUNKS:
+                continue
+            if n_chunk < PAIRED:
+                if n_chunk % 2 == 1:
+                    continue
+                both = keep.tile([P, 2 * 4 * N], U8, name="w%d_%d" % (w, g), align_bytes=256)
+                nc.sync.dma_start(
+                    out=both[:].bitcast(I32).rearrange("p (g m) -> p g m", g=2),
+                    in_=words[w][g : g + 2].rearrange("g p n t -> p g (n t)").bitcast(I32),
+                )
+                for j in range(2):
+                    for u, (c0, width) in enumerate(UNITS):
+                        w_tiles[(n_chunk + j, u)] = both[:, 4 * (N * j + c0) : 4 * (N * j + c0 + width)]
                 continue
             src = words[w][g].rearrange("p n t -> p (n t)")
             whole = keep.tile([P, 4 * N], U8, name="w%d_%d" % (w, g), align_bytes=256)

@@ -60,8 +60,9 @@ def tile_virtual16bmatmul_w_kernel(
 
         w_tiles = {}
         for n_chunk, (w, g) in enumerate(chunks):
-            if n_chunk == 2 or (n_chunk > 2 and n_chunk % 4 == 0):
-                load_scales(g // 4, w, (0, 1), nc.sync, I32)
+            if n_chunk == 2:
+                for block in range(4):
+                    load_scales(block // 2, block % 2, (0, 1), nc.sync, I32)
             if n_chunk >= len(chunks) - TAIL_CHUNKS:
                 continue
             if n_chunk < PAIRED:

@@ -60,9 +60,9 @@ def tile_virtual16bmatmul_w_kernel(
 
         w_tiles = {}
         for n_chunk, (w, g) in enumerate(chunks):
-            if n_chunk == 2:
-                for block in range(4):
-                    load_scales(block // 2, block % 2, (0, 1), nc.sync, I32)
+            if n_chunk in (2, 4):
+                for w_scale in range(2):
+                    load_scales(n_chunk // 2 - 1, w_scale, (0, 1), nc.sync, I32)
             if n_chunk >= len(chunks) - TAIL_CHUNKS:
                 continue
             if n_chunk < PAIRED:

from contextlib import ExitStack

import concourse.mybir as mybir
from concourse.masks import make_identity

F32 = mybir.dt.float32
BF16 = mybir.dt.bfloat16
I32 = mybir.dt.int32
U32 = mybir.dt.uint32
U8 = mybir.dt.uint8
FP8X4 = mybir.dt.float8_e4m3fn_x4

P = 128
K = 4096
N = 2048
GROUPS = K // 512
NT = 512
COLS = N // NT
FLOPS = 2 * 2 * P * K * N

UNITS = [(0, 512), (512, 512), (1024, 512), (1536, 256), (1792, 256)]
TAIL_CHUNKS = 2
PAIRED = 12
TAIL = [(14, 0, 2), (15, 0, 2), (14, 2, 1), (15, 2, 1), (14, 3, 2), (15, 3, 1), (15, 4, 1)]


def tile_virtual16bmatmul_w_kernel(
    tc, x, weight_upper_words, weight_upper_scales, weight_lower_words, weight_lower_scales, out
):
    nc = tc.nc
    x_rows = x.flatten_outer_dims()
    out_rows = out.flatten_outer_dims()
    words = [weight_upper_words, weight_lower_words]
    scales = [weight_upper_scales, weight_lower_scales]
    chunks = [(w, 4 * h + j) for h in range(2) for w in range(2) for j in range(4)]

    with ExitStack() as ctx:
        keep = ctx.enter_context(tc.tile_pool(name="keep", bufs=1))
        psum = ctx.enter_context(tc.psum_pool(name="psum", bufs=1))
        ctx.enter_context(tc.manual_schedule())

        planes = keep.tile([P, 4 * N], U8, name="planes", align_bytes=256)
        nc.vector.memset(planes[:].bitcast(I32), 0)
        ident = keep.tile([P, P], F32, name="ident", align_bytes=256)
        make_identity(nc, ident[:])

        x_sb = keep.tile([P, K], BF16, name="x_sb", align_bytes=256)
        nc.sync.dma_start(out=x_sb[:], in_=x_rows)

        def load_scales(h, w, quadrants, queue, view):
            i = 2 * h + w
            for q in quadrants:
                dst = planes[32 * q : 32 * q + 16, N * i : N * (i + 1)]
                src = scales[w][4 * h : 4 * h + 4, 4 * q : 4 * q + 4, :]
                queue.dma_start(out=dst.bitcast(view), in_=src.bitcast(view))

        for h in range(2):
            for w in range(2):
                load_scales(h, w, (2, 3), nc.gpsimd, F32)

        w_tiles = {}
        for n_chunk, (w, g) in enumerate(chunks):
            if n_chunk in (2, 4):
                for w_scale in range(2):
                    load_scales(n_chunk // 2 - 1, w_scale, (0, 1), nc.sync, I32)
            if n_chunk >= len(chunks) - TAIL_CHUNKS:
                continue
            if n_chunk < PAIRED:
                if n_chunk % 2 == 1:
                    continue
                both = keep.tile([P, 2 * 4 * N], U8, name="w%d_%d" % (w, g), align_bytes=256)
                nc.sync.dma_start(
                    out=both[:].bitcast(I32).rearrange("p (g m) -> p g m", g=2),
                    in_=words[w][g : g + 2].rearrange("g p n t -> p g (n t)").bitcast(I32),
                )
                for j in range(2):
                    for u, (c0, width) in enumerate(UNITS):
                        w_tiles[(n_chunk + j, u)] = both[:, 4 * (N * j + c0) : 4 * (N * j + c0 + width)]
                continue
            src = words[w][g].rearrange("p n t -> p (n t)")
            whole = keep.tile([P, 4 * N], U8, name="w%d_%d" % (w, g), align_bytes=256)
            nc.sync.dma_start(out=whole[:].bitcast(I32), in_=src.bitcast(I32))
            for u, (c0, width) in enumerate(UNITS):
                w_tiles[(n_chunk, u)] = whole[:, 4 * c0 : 4 * (c0 + width)]
        for n_chunk, u0, count in TAIL:
            w, g = chunks[n_chunk]
            src = words[w][g].rearrange("p n t -> p (n t)")
            first = UNITS[u0][0]
            cols = sum(UNITS[u][1] for u in range(u0, u0 + count))
            piece = keep.tile([P, 4 * cols], U8, name="wp%d_%d" % (n_chunk, u0), align_bytes=256)
            nc.sync.dma_start(out=piece[:].bitcast(I32), in_=src[:, 4 * first : 4 * (first + cols)].bitcast(I32))
            for u in range(u0, u0 + count):
                c0, width = UNITS[u]
                w_tiles[(n_chunk, u)] = piece[:, 4 * (c0 - first) : 4 * (c0 - first + width)]

        x_words = x_sb[:].bitcast(F32)
        grouped = keep.tile([P, K], BF16, name="grouped", align_bytes=256)
        grouped_words = grouped[:].bitcast(F32).rearrange("p (g m u) -> p g m u", g=GROUPS, m=P, u=2)
        x_codes = keep.tile([P, GROUPS * P], U32, name="x_codes", align_bytes=256)
        x_scales = keep.tile([P, GROUPS * P], U8, name="x_scales", align_bytes=256)
        banks = []
        for b in range(4):
            xt = psum.tile([P, 2, 2, P], F32, name="xt%d" % b)
            banks.append(xt)
            for gg in range(2):
                g = 2 * b + gg
                for u in range(2):
                    nc.tensor.transpose(xt[:, gg, u, :], x_words[:, 256 * g + u : 256 * (g + 1) : 2], ident[:])
        for b in (0, 2):
            nc.vector.tensor_copy(
                out=grouped_words[:, 2 * b : 2 * b + 2, :, :], in_=banks[b][:].rearrange("p g u m -> p g m u")
            )
        for b in (1, 3):
            nc.scalar.copy(
                out=grouped_words[:, 2 * b : 2 * b + 2, :, :], in_=banks[b][:].rearrange("p g u m -> p g m u")
            )
        for b in range(4):
            nc.vector.quantize_mx(
                out=x_codes[:, 256 * b : 256 * (b + 1)].bitcast(FP8X4),
                scales=x_scales[:, 256 * b : 256 * (b + 1)],
                in_=grouped[:, 1024 * b : 1024 * (b + 1)],
            )

        acc = [psum.tile([P, UNITS[u][1]], F32, name="acc%d" % u) for u in range(4)]
        acc.append(psum.tile([P, UNITS[4][1]], F32, name="acc4", tag="xt0"))

        def multiply(n_chunk, u):
            w, g = chunks[n_chunk]
            i = 2 * (g // 4) + w
            k_off = 4 * (g % 4)
            c0, width = UNITS[u]
            nc.tensor.matmul_mx(
                out=acc[u][:],
                lhsT=x_codes[:, P * g : P * (g + 1)].bitcast(FP8X4),
                lhsT_scale=x_scales[:, P * g : P * (g + 1)],
                rhs=w_tiles[(n_chunk, u)].bitcast(FP8X4),
                rhs_scale=planes[k_off:P, N * i + c0 : N * i + c0 + width],
                start=(n_chunk == 0),
                stop=(n_chunk == len(chunks) - 1),
            )

        for n_chunk in range(len(chunks) - TAIL_CHUNKS):
            for u in range(len(UNITS)):
                multiply(n_chunk, u)
        for n_chunk, u0, count in TAIL:
            for u in range(u0, u0 + count):
                multiply(n_chunk, u)
        for u, (c0, width) in enumerate(UNITS):
            res = keep.tile([P, width], F32, name="res%d" % u, align_bytes=256)
            if u % 2 == 0:
                nc.vector.tensor_copy(out=res[:], in_=acc[u][:])
            else:
                nc.scalar.copy(out=res[:], in_=acc[u][:])
            nc.sync.dma_start(out=out_rows[:, c0 : c0 + width], in_=res[:])
